import numpy as np
import ml_dtypes


def mxq(x, axis, fmt="e4m3"):
    dtype, down = {"e4m3": (ml_dtypes.float8_e4m3fn, 7), "e5m2": (ml_dtypes.float8_e5m2, 14)}[fmt]
    v = np.moveaxis(np.asarray(x, np.float32).astype(ml_dtypes.bfloat16).astype(np.float64), axis, -1)
    blocks = v.reshape(v.shape[:-1] + (-1, 32))
    amax = np.abs(blocks).max(-1, keepdims=True)
    byte = np.maximum(np.where(amax > 0, np.frexp(amax)[1] - 1 + 127, 0) - down, 1)
    scale = np.exp2(byte - 127.0)
    codes = (blocks / scale).astype(np.float32).astype(dtype).astype(np.float64)
    return np.moveaxis((codes * scale).reshape(v.shape), -1, axis)


WIDE = False


def mx_kscale(k):
    if not WIDE:
        return np.ones(k)
    levels = np.array([10, -10, 5, -5, 0])
    a = np.random.permutation(np.resize(levels, k // 512 * 4)).reshape(k // 512, 4)
    idx = np.arange(k)
    return np.exp2(a[idx // 512, idx % 128 // 32])


BF16 = ml_dtypes.bfloat16


def bf(x):
    return np.asarray(x, np.float32).astype(BF16)


def f64(x):
    return np.asarray(x).astype(np.float64)


B, N, D, P, Z = 8, 512, 1024, 511, 2
P1 = P + 1


def leaky_draw(shape):
    g = np.random.standard_normal(shape)
    return np.where(g > 0.0, g, 0.1 * g)


def with_ones(v):
    return np.concatenate([v, np.ones(v.shape[:-1] + (1,))], axis=-1)


def setup_inputs():
    s, u = mx_kscale(P1), mx_kscale(P1)
    s, u = s / s[-1], u / u[-1]
    return {"xp": bf(leaky_draw((B, N, P)) * s[:P]),
            "yp": bf(leaky_draw((B, N, P)) / u[:P]),
            "w": bf(np.random.standard_normal((B, Z, P1, P1)) * 0.36 / np.sqrt(P1) / s[:, None] * u)}


def reference(xp, yp, w):
    x1 = mxq(with_ones(f64(xp)), 2, "e4m3")
    y1 = mxq(with_ones(f64(yp)), 2, "e4m3")
    t = x1[:, None] @ mxq(f64(w), 2, "e4m3")
    sc = mxq(t, 3, "e4m3") @ y1.transpose(0, 2, 1)[:, None]
    return sc.transpose(0, 2, 3, 1)

@@ -1,0 +1,171 @@
+from contextlib import ExitStack
+
+import concourse.mybir as mybir
+from concourse.masks import make_identity
+
+BF16 = mybir.dt.bfloat16
+F32 = mybir.dt.float32
+U32 = mybir.dt.uint32
+U8 = mybir.dt.uint8
+FP8X4 = mybir.dt.float8_e4m3fn_x4
+
+B = 8
+Z = 2
+N = 512
+K = 512
+P = 128
+PACK = 4
+ROWS = N // P
+HALF = N // 2
+
+UNITS = B * ROWS
+RAW_SLOTS = 4
+PREP_LEAD = 6
+STAGE1_LEAD = 2
+
+FLOPS = 2 * 2 * B * Z * N * K * K
+
+
+def tile_span2oscorer_pa_t_kernel(tc, xp, yp, w, out):
+    nc = tc.nc
+    with ExitStack() as stack:
+        fixed = stack.enter_context(tc.tile_pool(name="fixed", bufs=1))
+        grouped = stack.enter_context(tc.tile_pool(name="grouped", bufs=3))
+        results = stack.enter_context(tc.tile_pool(name="results", bufs=8))
+        flip_banks = stack.enter_context(tc.psum_pool(name="flip_banks", bufs=2))
+        t_banks = stack.enter_context(tc.psum_pool(name="t_banks", bufs=3))
+        out_banks = stack.enter_context(tc.psum_pool(name="out_banks", bufs=3))
+        stack.enter_context(tc.manual_schedule())
+
+        identity = fixed.tile([P, P], F32)
+        make_identity(nc, identity[:])
+
+        x_raw = fixed.tile([P, RAW_SLOTS, ROWS, K], BF16)
+        y_raw = fixed.tile([P, RAW_SLOTS, ROWS, K], BF16)
+        w_raw = fixed.tile([P, RAW_SLOTS, Z, PACK, K], BF16)
+        nc.vector.memset(x_raw[:, :, :, K - 16 : K], 1.0)
+        nc.vector.memset(y_raw[:, :, :, K - 16 : K], 1.0)
+
+        x_codes = fixed.tile([P, 2, N], U32, align_bytes=64)
+        x_scales = fixed.tile([P, 2, N], U8, align_bytes=64)
+        y_codes = fixed.tile([P, 2, N], U32, align_bytes=64)
+        y_scales = fixed.tile([P, 2, N], U8, align_bytes=64)
+        w_codes = fixed.tile([P, 2, Z, K], U32, align_bytes=64)
+        w_scales = fixed.tile([P, 2, Z, K], U8, align_bytes=64)
+
+        def load(b):
+            slot = b % RAW_SLOTS
+            for z in range(Z):
+                nc.sync.dma_start(
+                    out=w_raw[:, slot, z].rearrange("p (u e) j -> p u e j", u=2),
+                    in_=w[b, z].rearrange("(u p e) j -> p u e j", u=2, e=2),
+                )
+                if z == 0:
+                    nc.sync.dma_start(
+                        out=x_raw[:, slot, :, 0 : K - 1], in_=xp[b].rearrange("(m r) k -> m r k", r=ROWS)
+                    )
+            nc.sync.dma_start(out=y_raw[:, slot, :, 0 : K - 1], in_=yp[b].rearrange("(r m) k -> m r k", r=ROWS))
+
+        def prepare(piece):
+            b, quarter = divmod(piece, ROWS)
+            slot, parity = b % RAW_SLOTS, b % 2
+            first, half = divmod(quarter, 2)
+            cols = slice(half * HALF, (half + 1) * HALF)
+
+            raw, codes, scales = ((x_raw, x_codes, x_scales), (y_raw, y_codes, y_scales))[first]
+            words = raw[:, slot].bitcast(F32)
+            flipped = flip_banks.tile([P, 2, 2, P], F32)
+            for pair_row in range(2):
+                for u in range(2):
+                    nc.tensor.transpose(
+                        flipped[:, pair_row, u, :], words[:, 2 * half + pair_row, u * P : (u + 1) * P], identity[:]
+                    )
+            xy_grouped = grouped.tile([P, 2, P, PACK], BF16, align_bytes=64)
+            nc.scalar.copy(out=xy_grouped[:].bitcast(F32), in_=flipped[:].rearrange("p r u m -> p r m u"))
+
+            w_grouped = grouped.tile([P, 2, P, PACK], BF16, align_bytes=64)
+            nc.vector.tensor_copy(
+                out=w_grouped[:], in_=w_raw[:, slot, first, :, cols].rearrange("p t (q e) -> p e q t", e=2)
+            )
+            nc.vector.quantize_mx(
+                out=codes[:, parity, cols].bitcast(FP8X4),
+                scales=scales[:, parity, cols],
+                in_=xy_grouped[:].rearrange("p r m t -> p (r m t)"),
+            )
+            nc.vector.quantize_mx(
+                out=w_codes[:, parity, first, cols].bitcast(FP8X4),
+                scales=w_scales[:, parity, first, cols],
+                in_=w_grouped[:].rearrange("p e q t -> p (e q t)"),
+            )
+            if quarter == ROWS - 1 and b + RAW_SLOTS < B:
+                load(b + RAW_SLOTS)
+
+        t_grouped = {}
+        t_quantised = {}
+
+        def stage1(unit):
+            b, r = divmod(unit, ROWS)
+            parity = b % 2
+            t_grouped[unit] = grouped.tile([P, Z, P, PACK], BF16, align_bytes=64, name="t_grouped")
+            for z in range(Z):
+                t_bank = t_banks.tile([P, PACK, P], F32)
+                for t in range(PACK):
+                    nc.tensor.matmul_mx(
+                        out=t_bank[:, t, :],
+                        lhsT=w_codes[:, parity, z, t * P : (t + 1) * P].bitcast(FP8X4),
+                        lhsT_scale=w_scales[:, parity, z, t * P : (t + 1) * P],
+                        rhs=x_codes[:, parity, r * P : (r + 1) * P].bitcast(FP8X4),
+                        rhs_scale=x_scales[:, parity, r * P : (r + 1) * P],
+                        start=True,
+                        stop=True,
+                    )
+                nc.scalar.copy(out=t_grouped[unit][:, z], in_=t_bank[:].rearrange("p t m -> p m t"))
+
+        def quantise_t(unit):
+            t_codes = grouped.tile([P, Z * P], U32, align_bytes=64)
+            t_scales = grouped.tile([P, Z * P], U8, align_bytes=64)
+            nc.vector.quantize_mx(
+                out=t_codes[:].bitcast(FP8X4),
+                scales=t_scales[:],
+                in_=t_grouped[unit][:].rearrange("p z m t -> p (z m t)"),
+            )
+            t_quantised[unit] = (t_codes, t_scales)
+
+        def stage2(unit):
+            b, r = divmod(unit, ROWS)
+            parity = b % 2
+            t_codes, t_scales = t_quantised[unit]
+            result = results.tile([P, N, Z], F32)
+            for half in range(2):
+                cols = slice(half * HALF, (half + 1) * HALF)
+                out_bank = out_banks.tile([P, Z, HALF], F32)
+                for z in range(Z):
+                    nc.tensor.matmul_mx(
+                        out=out_bank[:, z, :],
+                        lhsT=t_codes[:, z * P : (z + 1) * P].bitcast(FP8X4),
+                        lhsT_scale=t_scales[:, z * P : (z + 1) * P],
+                        rhs=y_codes[:, parity, cols].bitcast(FP8X4),
+                        rhs_scale=y_scales[:, parity, cols],
+                        start=True,
+                        stop=True,
+                    )
+                if half == 0:
+                    nc.scalar.copy(out=result[:, cols, :], in_=out_bank[:].rearrange("p z y -> p y z"))
+                else:
+                    nc.vector.tensor_copy(out=result[:, cols, :], in_=out_bank[:].rearrange("p z y -> p y z"))
+            nc.sync.dma_start(
+                out=out[b].rearrange("(m r) y z -> m r (y z)", r=ROWS)[:, r, :],
+                in_=result[:].rearrange("p y z -> p (y z)"),
+            )
+
+        for b in range(RAW_SLOTS):
+            load(b)
+        for step in range(-PREP_LEAD, UNITS):
+            if 0 <= step + STAGE1_LEAD - 1 < UNITS:
+                quantise_t(step + STAGE1_LEAD - 1)
+            if step + PREP_LEAD < UNITS:
+                prepare(step + PREP_LEAD)
+            if 0 <= step + STAGE1_LEAD < UNITS:
+                stage1(step + STAGE1_LEAD)
+            if step >= 0:
+                stage2(step)

@@ -20,6 +20,7 @@ HALF = N // 2
 
 UNITS = B * ROWS
 RAW_SLOTS = 4
+RESULT_SLOTS = 16
 PREP_LEAD = 6
 STAGE1_LEAD = 2
 
@@ -31,7 +32,7 @@ def tile_span2oscorer_pa_t_kernel(tc, xp, yp, w, out):
     with ExitStack() as stack:
         fixed = stack.enter_context(tc.tile_pool(name="fixed", bufs=1))
         grouped = stack.enter_context(tc.tile_pool(name="grouped", bufs=3))
-        results = stack.enter_context(tc.tile_pool(name="results", bufs=8))
+        results = stack.enter_context(tc.tile_pool(name="results", bufs=RESULT_SLOTS))
         flip_banks = stack.enter_context(tc.psum_pool(name="flip_banks", bufs=2))
         t_banks = stack.enter_context(tc.psum_pool(name="t_banks", bufs=3))
         out_banks = stack.enter_context(tc.psum_pool(name="out_banks", bufs=3))

@@ -20,9 +20,9 @@ HALF = N // 2
 
 UNITS = B * ROWS
 RAW_SLOTS = 4
-RESULT_SLOTS = 16
-PREP_LEAD = 6
-STAGE1_LEAD = 2
+RESULT_SLOTS = 4
+PREP_LEAD = 7
+STAGE1_LEAD = 3
 
 FLOPS = 2 * 2 * B * Z * N * K * K
 
@@ -31,7 +31,7 @@ def tile_span2oscorer_pa_t_kernel(tc, xp, yp, w, out):
     nc = tc.nc
     with ExitStack() as stack:
         fixed = stack.enter_context(tc.tile_pool(name="fixed", bufs=1))
-        grouped = stack.enter_context(tc.tile_pool(name="grouped", bufs=3))
+        grouped = stack.enter_context(tc.tile_pool(name="grouped", bufs=4))
         results = stack.enter_context(tc.tile_pool(name="results", bufs=RESULT_SLOTS))
         flip_banks = stack.enter_context(tc.psum_pool(name="flip_banks", bufs=2))
         t_banks = stack.enter_context(tc.psum_pool(name="t_banks", bufs=3))
@@ -56,53 +56,61 @@ def tile_span2oscorer_pa_t_kernel(tc, xp, yp, w, out):
 
         def load(b):
             slot = b % RAW_SLOTS
+            nc.sync.dma_start(out=x_raw[:, slot, :, 0 : K - 1], in_=xp[b].rearrange("(m r) k -> m r k", r=ROWS))
             for z in range(Z):
                 nc.sync.dma_start(
                     out=w_raw[:, slot, z].rearrange("p (u e) j -> p u e j", u=2),
                     in_=w[b, z].rearrange("(u p e) j -> p u e j", u=2, e=2),
                 )
-                if z == 0:
-                    nc.sync.dma_start(
-                        out=x_raw[:, slot, :, 0 : K - 1], in_=xp[b].rearrange("(m r) k -> m r k", r=ROWS)
-                    )
             nc.sync.dma_start(out=y_raw[:, slot, :, 0 : K - 1], in_=yp[b].rearrange("(r m) k -> m r k", r=ROWS))
 
-        def prepare(piece):
+        def piece_of(piece):
             b, quarter = divmod(piece, ROWS)
-            slot, parity = b % RAW_SLOTS, b % 2
-            first, half = divmod(quarter, 2)
-            cols = slice(half * HALF, (half + 1) * HALF)
+            z, half = divmod(quarter, 2)
+            return b, z, half, slice(half * HALF, (half + 1) * HALF)
 
-            raw, codes, scales = ((x_raw, x_codes, x_scales), (y_raw, y_codes, y_scales))[first]
-            words = raw[:, slot].bitcast(F32)
+        xy_grouped = {}
+        w_grouped = {}
+
+        def flip_xy(piece):
+            b, z, half, cols = piece_of(piece)
+            words = (x_raw, y_raw)[z][:, b % RAW_SLOTS].bitcast(F32)
             flipped = flip_banks.tile([P, 2, 2, P], F32)
             for pair_row in range(2):
                 for u in range(2):
                     nc.tensor.transpose(
                         flipped[:, pair_row, u, :], words[:, 2 * half + pair_row, u * P : (u + 1) * P], identity[:]
                     )
-            xy_grouped = grouped.tile([P, 2, P, PACK], BF16, align_bytes=64)
-            nc.scalar.copy(out=xy_grouped[:].bitcast(F32), in_=flipped[:].rearrange("p r u m -> p r m u"))
+            xy_grouped[piece] = grouped.tile([P, 2, P, PACK], BF16, align_bytes=64, name="xy_grouped")
+            nc.scalar.copy(out=xy_grouped[piece][:].bitcast(F32), in_=flipped[:].rearrange("p r u m -> p r m u"))
 
-            w_grouped = grouped.tile([P, 2, P, PACK], BF16, align_bytes=64)
+        def regroup_w(piece):
+            b, z, half, cols = piece_of(piece)
+            w_grouped[piece] = grouped.tile([P, 2, P, PACK], BF16, align_bytes=64, name="w_grouped")
             nc.vector.tensor_copy(
-                out=w_grouped[:], in_=w_raw[:, slot, first, :, cols].rearrange("p t (q e) -> p e q t", e=2)
+                out=w_grouped[piece][:],
+                in_=w_raw[:, b % RAW_SLOTS, z, :, cols].rearrange("p t (q e) -> p e q t", e=2),
+            )
+
+        def quantise_inputs(piece):
+            b, z, half, cols = piece_of(piece)
+            parity = b % 2
+            nc.vector.quantize_mx(
+                out=(x_codes, y_codes)[z][:, parity, cols].bitcast(FP8X4),
+                scales=(x_scales, y_scales)[z][:, parity, cols],
+                in_=xy_grouped[piece][:].rearrange("p r m t -> p (r m t)"),
             )
             nc.vector.quantize_mx(
-                out=codes[:, parity, cols].bitcast(FP8X4),
-                scales=scales[:, parity, cols],
-                in_=xy_grouped[:].rearrange("p r m t -> p (r m t)"),
+                out=w_codes[:, parity, z, cols].bitcast(FP8X4),
+                scales=w_scales[:, parity, z, cols],
+                in_=w_grouped[piece][:].rearrange("p e q t -> p (e q t)"),
             )
-            nc.vector.quantize_mx(
-                out=w_codes[:, parity, first, cols].bitcast(FP8X4),
-                scales=w_scales[:, parity, first, cols],
-                in_=w_grouped[:].rearrange("p e q t -> p (e q t)"),
-            )
-            if quarter == ROWS - 1 and b + RAW_SLOTS < B:
+            if piece % ROWS == ROWS - 1 and b + RAW_SLOTS < B:
                 load(b + RAW_SLOTS)
 
         t_grouped = {}
         t_quantised = {}
+        result = {}
 
         def stage1(unit):
             b, r = divmod(unit, ROWS)
@@ -136,7 +144,8 @@ def tile_span2oscorer_pa_t_kernel(tc, xp, yp, w, out):
             b, r = divmod(unit, ROWS)
             parity = b % 2
             t_codes, t_scales = t_quantised[unit]
-            result = results.tile([P, N, Z], F32)
+            if r == 0:
+                result[b] = results.tile([P, ROWS, N, Z], F32, name="result")
             for half in range(2):
                 cols = slice(half * HALF, (half + 1) * HALF)
                 out_bank = out_banks.tile([P, Z, HALF], F32)
@@ -151,22 +160,27 @@ def tile_span2oscorer_pa_t_kernel(tc, xp, yp, w, out):
                         stop=True,
                     )
                 if half == 0:
-                    nc.scalar.copy(out=result[:, cols, :], in_=out_bank[:].rearrange("p z y -> p y z"))
+                    nc.scalar.copy(out=result[b][:, r, cols, :], in_=out_bank[:].rearrange("p z y -> p y z"))
                 else:
-                    nc.vector.tensor_copy(out=result[:, cols, :], in_=out_bank[:].rearrange("p z y -> p y z"))
-            nc.sync.dma_start(
-                out=out[b].rearrange("(m r) y z -> m r (y z)", r=ROWS)[:, r, :],
-                in_=result[:].rearrange("p y z -> p (y z)"),
-            )
+                    nc.vector.tensor_copy(out=result[b][:, r, cols, :], in_=out_bank[:].rearrange("p z y -> p y z"))
+            rows_of_out = out[b].rearrange("(m r) y z -> m r (y z)", r=ROWS)
+            rows_of_result = result[b][:].rearrange("p r y z -> p r (y z)")
+            if b == B - 1:
+                nc.sync.dma_start(out=rows_of_out[:, r, :], in_=rows_of_result[:, r, :])
+            elif r == ROWS - 1:
+                nc.sync.dma_start(out=rows_of_out, in_=rows_of_result)
 
         for b in range(RAW_SLOTS):
             load(b)
         for step in range(-PREP_LEAD, UNITS):
             if 0 <= step + STAGE1_LEAD - 1 < UNITS:
                 quantise_t(step + STAGE1_LEAD - 1)
-            if step + PREP_LEAD < UNITS:
-                prepare(step + PREP_LEAD)
             if 0 <= step + STAGE1_LEAD < UNITS:
                 stage1(step + STAGE1_LEAD)
+            if step + PREP_LEAD < UNITS:
+                flip_xy(step + PREP_LEAD)
+                regroup_w(step + PREP_LEAD)
             if step >= 0:
                 stage2(step)
+            if step + PREP_LEAD < UNITS:
+                quantise_inputs(step + PREP_LEAD)

from contextlib import ExitStack

import concourse.mybir as mybir
from concourse.masks import make_identity

BF16 = mybir.dt.bfloat16
F32 = mybir.dt.float32
U32 = mybir.dt.uint32
U8 = mybir.dt.uint8
FP8X4 = mybir.dt.float8_e4m3fn_x4

B = 8
Z = 2
N = 512
K = 512
P = 128
PACK = 4
ROWS = N // P
HALF = N // 2

UNITS = B * ROWS
RAW_SLOTS = 4
RESULT_SLOTS = 4
PREP_LEAD = 7
STAGE1_LEAD = 3

FLOPS = 2 * 2 * B * Z * N * K * K


def tile_span2oscorer_pa_t_kernel(tc, xp, yp, w, out):
    nc = tc.nc
    with ExitStack() as stack:
        fixed = stack.enter_context(tc.tile_pool(name="fixed", bufs=1))
        grouped = stack.enter_context(tc.tile_pool(name="grouped", bufs=4))
        results = stack.enter_context(tc.tile_pool(name="results", bufs=RESULT_SLOTS))
        flip_banks = stack.enter_context(tc.psum_pool(name="flip_banks", bufs=2))
        t_banks = stack.enter_context(tc.psum_pool(name="t_banks", bufs=3))
        out_banks = stack.enter_context(tc.psum_pool(name="out_banks", bufs=3))
        stack.enter_context(tc.manual_schedule())

        identity = fixed.tile([P, P], F32)
        make_identity(nc, identity[:])

        x_raw = fixed.tile([P, RAW_SLOTS, ROWS, K], BF16)
        y_raw = fixed.tile([P, RAW_SLOTS, ROWS, K], BF16)
        w_raw = fixed.tile([P, RAW_SLOTS, Z, PACK, K], BF16)
        nc.vector.memset(x_raw[:, :, :, K - 16 : K], 1.0)
        nc.vector.memset(y_raw[:, :, :, K - 16 : K], 1.0)

        x_codes = fixed.tile([P, 2, N], U32, align_bytes=64)
        x_scales = fixed.tile([P, 2, N], U8, align_bytes=64)
        y_codes = fixed.tile([P, 2, N], U32, align_bytes=64)
        y_scales = fixed.tile([P, 2, N], U8, align_bytes=64)
        w_codes = fixed.tile([P, 2, Z, K], U32, align_bytes=64)
        w_scales = fixed.tile([P, 2, Z, K], U8, align_bytes=64)

        def load(b):
            slot = b % RAW_SLOTS
            nc.sync.dma_start(out=x_raw[:, slot, :, 0 : K - 1], in_=xp[b].rearrange("(m r) k -> m r k", r=ROWS))
            for z in range(Z):
                nc.sync.dma_start(
                    out=w_raw[:, slot, z].rearrange("p (u e) j -> p u e j", u=2),
                    in_=w[b, z].rearrange("(u p e) j -> p u e j", u=2, e=2),
                )
            nc.sync.dma_start(out=y_raw[:, slot, :, 0 : K - 1], in_=yp[b].rearrange("(r m) k -> m r k", r=ROWS))

        def piece_of(piece):
            b, quarter = divmod(piece, ROWS)
            z, half = divmod(quarter, 2)
            return b, z, half, slice(half * HALF, (half + 1) * HALF)

        xy_grouped = {}
        w_grouped = {}

        def flip_xy(piece):
            b, z, half, cols = piece_of(piece)
            words = (x_raw, y_raw)[z][:, b % RAW_SLOTS].bitcast(F32)
            flipped = flip_banks.tile([P, 2, 2, P], F32)
            for pair_row in range(2):
                for u in range(2):
                    nc.tensor.transpose(
                        flipped[:, pair_row, u, :], words[:, 2 * half + pair_row, u * P : (u + 1) * P], identity[:]
                    )
            xy_grouped[piece] = grouped.tile([P, 2, P, PACK], BF16, align_bytes=64, name="xy_grouped")
            nc.scalar.copy(out=xy_grouped[piece][:].bitcast(F32), in_=flipped[:].rearrange("p r u m -> p r m u"))

        def regroup_w(piece):
            b, z, half, cols = piece_of(piece)
            w_grouped[piece] = grouped.tile([P, 2, P, PACK], BF16, align_bytes=64, name="w_grouped")
            nc.vector.tensor_copy(
                out=w_grouped[piece][:],
                in_=w_raw[:, b % RAW_SLOTS, z, :, cols].rearrange("p t (q e) -> p e q t", e=2),
            )

        def quantise_inputs(piece):
            b, z, half, cols = piece_of(piece)
            parity = b % 2
            nc.vector.quantize_mx(
                out=(x_codes, y_codes)[z][:, parity, cols].bitcast(FP8X4),
                scales=(x_scales, y_scales)[z][:, parity, cols],
                in_=xy_grouped[piece][:].rearrange("p r m t -> p (r m t)"),
            )
            nc.vector.quantize_mx(
                out=w_codes[:, parity, z, cols].bitcast(FP8X4),
                scales=w_scales[:, parity, z, cols],
                in_=w_grouped[piece][:].rearrange("p e q t -> p (e q t)"),
            )
            if piece % ROWS == ROWS - 1 and b + RAW_SLOTS < B:
                load(b + RAW_SLOTS)

        t_grouped = {}
        t_quantised = {}
        result = {}

        def stage1(unit):
            b, r = divmod(unit, ROWS)
            parity = b % 2
            t_grouped[unit] = grouped.tile([P, Z, P, PACK], BF16, align_bytes=64, name="t_grouped")
            for z in range(Z):
                t_bank = t_banks.tile([P, PACK, P], F32)
                for t in range(PACK):
                    nc.tensor.matmul_mx(
                        out=t_bank[:, t, :],
                        lhsT=w_codes[:, parity, z, t * P : (t + 1) * P].bitcast(FP8X4),
                        lhsT_scale=w_scales[:, parity, z, t * P : (t + 1) * P],
                        rhs=x_codes[:, parity, r * P : (r + 1) * P].bitcast(FP8X4),
                        rhs_scale=x_scales[:, parity, r * P : (r + 1) * P],
                        start=True,
                        stop=True,
                    )
                nc.scalar.copy(out=t_grouped[unit][:, z], in_=t_bank[:].rearrange("p t m -> p m t"))

        def quantise_t(unit):
            t_codes = grouped.tile([P, Z * P], U32, align_bytes=64)
            t_scales = grouped.tile([P, Z * P], U8, align_bytes=64)
            nc.vector.quantize_mx(
                out=t_codes[:].bitcast(FP8X4),
                scales=t_scales[:],
                in_=t_grouped[unit][:].rearrange("p z m t -> p (z m t)"),
            )
            t_quantised[unit] = (t_codes, t_scales)

        def stage2(unit):
            b, r = divmod(unit, ROWS)
            parity = b % 2
            t_codes, t_scales = t_quantised[unit]
            if r == 0:
                result[b] = results.tile([P, ROWS, N, Z], F32, name="result")
            for half in range(2):
                cols = slice(half * HALF, (half + 1) * HALF)
                out_bank = out_banks.tile([P, Z, HALF], F32)
                for z in range(Z):
                    nc.tensor.matmul_mx(
                        out=out_bank[:, z, :],
                        lhsT=t_codes[:, z * P : (z + 1) * P].bitcast(FP8X4),
                        lhsT_scale=t_scales[:, z * P : (z + 1) * P],
                        rhs=y_codes[:, parity, cols].bitcast(FP8X4),
                        rhs_scale=y_scales[:, parity, cols],
                        start=True,
                        stop=True,
                    )
                if half == 0:
                    nc.scalar.copy(out=result[b][:, r, cols, :], in_=out_bank[:].rearrange("p z y -> p y z"))
                else:
                    nc.vector.tensor_copy(out=result[b][:, r, cols, :], in_=out_bank[:].rearrange("p z y -> p y z"))
            rows_of_out = out[b].rearrange("(m r) y z -> m r (y z)", r=ROWS)
            rows_of_result = result[b][:].rearrange("p r y z -> p r (y z)")
            if b == B - 1:
                nc.sync.dma_start(out=rows_of_out[:, r, :], in_=rows_of_result[:, r, :])
            elif r == ROWS - 1:
                nc.sync.dma_start(out=rows_of_out, in_=rows_of_result)

        for b in range(RAW_SLOTS):
            load(b)
        for step in range(-PREP_LEAD, UNITS):
            if 0 <= step + STAGE1_LEAD - 1 < UNITS:
                quantise_t(step + STAGE1_LEAD - 1)
            if 0 <= step + STAGE1_LEAD < UNITS:
                stage1(step + STAGE1_LEAD)
            if step + PREP_LEAD < UNITS:
                flip_xy(step + PREP_LEAD)
                regroup_w(step + PREP_LEAD)
            if step >= 0:
                stage2(step)
            if step + PREP_LEAD < UNITS:
                quantise_inputs(step + PREP_LEAD)
